import numpy as np
import ml_dtypes


def mxq(x, axis, fmt="e4m3"):
    dtype, down = {"e4m3": (ml_dtypes.float8_e4m3fn, 7), "e5m2": (ml_dtypes.float8_e5m2, 14)}[fmt]
    v = np.moveaxis(np.asarray(x, np.float32).astype(ml_dtypes.bfloat16).astype(np.float64), axis, -1)
    blocks = v.reshape(v.shape[:-1] + (-1, 32))
    amax = np.abs(blocks).max(-1, keepdims=True)
    byte = np.maximum(np.where(amax > 0, np.frexp(amax)[1] - 1 + 127, 0) - down, 1)
    scale = np.exp2(byte - 127.0)
    codes = (blocks / scale).astype(np.float32).astype(dtype).astype(np.float64)
    return np.moveaxis((codes * scale).reshape(v.shape), -1, axis)


WIDE = False


def mx_kscale(k):
    if not WIDE:
        return np.ones(k)
    levels = np.array([10, -10, 5, -5, 0])
    if k % 512:
        return np.exp2(np.random.permutation(np.resize(levels, k // 32))).repeat(32)
    a = np.empty((k // 512, 16))
    for p in range(k // 512):
        a[p, :8] = np.random.permutation(np.resize(levels, 8))
        for g in range(8):
            far = levels[np.abs(levels - a[p, g]) >= 10]
            a[p, g + 8] = far[np.random.randint(len(far))]
    return np.exp2(a.ravel()).repeat(32)


BF16 = ml_dtypes.bfloat16


def bf(x):
    return np.asarray(x, np.float32).astype(BF16)


def f64(x):
    return np.asarray(x).astype(np.float64)


B, H, W, C = 128, 5, 5, 1024
PIXEL = 2
STEP = 1
EPS = 1e-6
PAD = (PIXEL - H % PIXEL) % PIXEL
HP = H + PAD
R = HP // PIXEL
K1 = PIXEL * C
F = C // 2


def layer_norm(v, g, b):
    m = v.mean(-1, keepdims=True)
    var = np.square(v - m).mean(-1, keepdims=True)
    return (v - m) / np.sqrt(var + EPS) * g + b


def setup_inputs():
    s = mx_kscale(C)
    t = mx_kscale(F)
    return {
        "x": bf(np.random.standard_normal((B, H, W, C)) * s),
        "wh1": bf(np.random.standard_normal((K1, F)) / np.sqrt(K1) / np.tile(s, PIXEL)[:, None]),
        "gh": bf((1.0 + 0.1 * np.random.standard_normal(F)) * t),
        "bh": bf(0.2 * np.random.standard_normal(F) * t),
        "wh2": bf(np.random.standard_normal((F, K1)) / np.sqrt(F) / t[:, None]),
        "bh2": bf(0.3 * np.random.standard_normal(K1)),
    }


def reference(x, wh1, gh, bh, wh2, bh2):
    r = np.roll(f64(x), STEP, axis=1)
    r = np.concatenate([r[:, -PAD:], r], axis=1)
    z = r.reshape(B, PIXEL, R, W, C).transpose(0, 2, 3, 1, 4).reshape(B, R, W, K1)
    u = mxq(z, 3, "e4m3") @ mxq(f64(wh1), 0, "e4m3")
    hid = np.maximum(layer_norm(u, f64(gh), f64(bh)), 0.0)
    y = (mxq(hid, 3, "e4m3") @ mxq(f64(wh2), 0, "e4m3")) + f64(bh2)
    y = y.reshape(B, R, W, PIXEL, C).transpose(0, 3, 1, 2, 4).reshape(B, HP, W, C)[:, PAD:]
    return np.roll(y, -STEP, axis=1)

@@ -1,0 +1,289 @@
+from contextlib import ExitStack
+
+import concourse.mybir as mybir
+from concourse.masks import make_identity
+
+F32 = mybir.dt.float32
+BF16 = mybir.dt.bfloat16
+U32 = mybir.dt.uint32
+U8 = mybir.dt.uint8
+FP8X4 = mybir.dt.float8_e4m3fn_x4
+ACT = mybir.ActivationFunctionType
+ALU = mybir.AluOpType
+
+P = 128
+PACK = 4
+K_PASS = P * PACK
+N_TILE = 512
+
+B, H, W, C = 128, 5, 5, 1024
+PIXEL = 2
+R = 3
+K1 = PIXEL * C
+F = C // 2
+EPS = 1e-6
+ROW_PASSES = C // K_PASS
+W1_PASSES = K1 // K_PASS
+W2_BLOCKS = K1 // N_TILE
+ROW_BLOCKS = C // N_TILE
+
+FLOPS = 2 * B * R * W * (K1 * F + F * K1)
+
+
+def image_row(j, pixel):
+    return (j + R * pixel + 3) % H
+
+
+def tile_hiremodule_pa_kernel(tc, x, wh1, gh, bh, wh2, bh2, out):
+    nc = tc.nc
+    regions = [(w, j) for w in range(W) for j in range(R)]
+    with ExitStack() as ctx:
+        ctx.enter_context(tc.manual_schedule())
+        consts = ctx.enter_context(tc.tile_pool(name="consts", bufs=1))
+        x_pool = ctx.enter_context(tc.tile_pool(name="x_pool", bufs=H * W))
+        stage = ctx.enter_context(tc.tile_pool(name="stage", bufs=3))
+        work = ctx.enter_context(tc.tile_pool(name="work", bufs=3))
+        x_code_pool = ctx.enter_context(tc.tile_pool(name="x_code_pool", bufs=2 * H))
+        out_pool = ctx.enter_context(tc.tile_pool(name="out_pool", bufs=6))
+        psum_x = ctx.enter_context(tc.psum_pool(name="psum_x", bufs=2))
+        psum_u = ctx.enter_context(tc.psum_pool(name="psum_u", bufs=2))
+        psum_h = ctx.enter_context(tc.psum_pool(name="psum_h", bufs=1))
+        psum_y = ctx.enter_context(tc.psum_pool(name="psum_y", bufs=3))
+
+        def new_rows(j):
+            rows = [image_row(j, pixel) for pixel in range(PIXEL)]
+            return [h for h in rows if j == 0 or h != image_row(0, 0)]
+
+        x_rows = {}
+
+        def load_x(w):
+            for j in range(R):
+                for h in new_rows(j):
+                    x_row = x_pool.tile([P, C], BF16)
+                    nc.sync.dma_start(out=x_row[:], in_=x[:, h, w, :])
+                    x_rows[(w, h)] = x_row
+
+        gain_raw = consts.tile([P, PACK], BF16)
+        nc.sync.dma_start(out=gain_raw[:], in_=gh.rearrange("(p t) -> p t", t=PACK))
+        shift_raw = consts.tile([P, PACK], BF16)
+        nc.sync.dma_start(out=shift_raw[:], in_=bh.rearrange("(p t) -> p t", t=PACK))
+        w1_raw = consts.tile([P, W1_PASSES, PACK, F], BF16)
+        for c in range(W1_PASSES):
+            nc.sync.dma_start(
+                out=w1_raw[:, c],
+                in_=wh1[c * K_PASS : (c + 1) * K_PASS, :].rearrange("(p t) f -> p t f", t=PACK),
+            )
+        load_x(0)
+        w2_order = [(k + W2_BLOCKS // 2) % W2_BLOCKS for k in range(W2_BLOCKS)]
+        w2_raw = consts.tile([P, W2_BLOCKS, PACK, N_TILE], BF16)
+
+        def load_w2(blocks):
+            for n in blocks:
+                nc.sync.dma_start(
+                    out=w2_raw[:, n],
+                    in_=wh2[:, n * N_TILE : (n + 1) * N_TILE].rearrange("(p t) c -> p t c", t=PACK),
+                )
+
+        load_w2(w2_order[: W2_BLOCKS // 2])
+        load_x(1)
+        load_w2(w2_order[W2_BLOCKS // 2 :])
+        bias2 = consts.tile([P, K1], BF16)
+        nc.sync.dma_start(out=bias2[:], in_=bh2.partition_broadcast(P))
+        for w in range(2, W):
+            load_x(w)
+
+        ident = consts.tile([P, P], F32)
+        make_identity(nc, ident[:])
+        eps = consts.tile([P, 1], F32)
+        nc.vector.memset(eps[:], EPS)
+
+        gain_cols = consts.tile([P, 2 * PACK], F32)
+        nc.vector.tensor_copy(out=gain_cols[:, 0:PACK], in_=gain_raw[:])
+        nc.vector.tensor_copy(out=gain_cols[:, PACK : 2 * PACK], in_=shift_raw[:])
+
+        def regroup_weight_block(raw):
+            grouped = stage.tile([P, N_TILE, PACK], BF16, align_bytes=64, tag="w_grouped")
+            half = N_TILE // 2
+            nc.vector.tensor_copy(
+                out=grouped[:, :half, :].rearrange("p (c i) t -> p c t i", i=4),
+                in_=raw[:, :, :half].rearrange("p t (c i) -> p c t i", i=4),
+            )
+            nc.scalar.copy(
+                out=grouped[:, half:, :].rearrange("p (c i) t -> p c t i", i=4),
+                in_=raw[:, :, half:].rearrange("p t (c i) -> p c t i", i=4),
+            )
+            return grouped
+
+        def quantise_weight_block(grouped, codes, scales):
+            nc.vector.quantize_mx(
+                out=codes.bitcast(FP8X4),
+                scales=scales,
+                in_=grouped[:].rearrange("p c t -> p (c t)"),
+            )
+
+        w1_codes = consts.tile([P, W1_PASSES, F], U32, align_bytes=64)
+        w1_scales = consts.tile([P, W1_PASSES, F], U8, align_bytes=64)
+        w1_grouped = {}
+        for c in range(W1_PASSES + 1):
+            if c < W1_PASSES:
+                w1_grouped[c] = regroup_weight_block(w1_raw[:, c])
+            if c > 0:
+                quantise_weight_block(w1_grouped[c - 1], w1_codes[:, c - 1, :], w1_scales[:, c - 1, :])
+        w2_codes = consts.tile([P, W2_BLOCKS, N_TILE], U32, align_bytes=64)
+        w2_scales = consts.tile([P, W2_BLOCKS, N_TILE], U8, align_bytes=64)
+
+        x_t, x_grouped, x_codes, x_scales = {}, {}, {}, {}
+        u_bank, mean_var, norms, hid_ts, hid_planes, hid_codes, hid_scales = {}, {}, {}, {}, {}, {}, {}
+
+        def transpose_x(n):
+            w, j = regions[n]
+            for h in new_rows(j):
+                x_words = x_rows[(w, h)][:].bitcast(F32)
+                bank = psum_x.tile([P, 2 * ROW_PASSES, P], F32)
+                for q in range(2 * ROW_PASSES):
+                    first = (q // 2) * 2 * P + q % 2
+                    nc.tensor.transpose(
+                        bank[:, q, :], x_words[:, first : first + 2 * P - 1 : 2], ident[:]
+                    )
+                x_t[(w, h)] = bank
+
+        def copy_x(n):
+            w, j = regions[n]
+            for h in new_rows(j):
+                grouped = stage.tile([P, ROW_PASSES, P, 2], F32, align_bytes=64, tag="x_grouped")
+                nc.scalar.copy(
+                    out=grouped[:], in_=x_t[(w, h)][:].rearrange("p (g u) b -> p g b u", u=2)
+                )
+                x_grouped[(w, h)] = grouped
+
+        def quantise_x(n):
+            w, j = regions[n]
+            for h in new_rows(j):
+                codes = x_code_pool.tile([P, ROW_PASSES, P], U32, align_bytes=64, tag="x_codes")
+                scales = x_code_pool.tile([P, ROW_PASSES, P], U8, align_bytes=64, tag="x_scales")
+                nc.vector.quantize_mx(
+                    out=codes[:].rearrange("p g b -> p (g b)").bitcast(FP8X4),
+                    scales=scales[:].rearrange("p g b -> p (g b)"),
+                    in_=x_grouped[(w, h)][:].rearrange("p g b u -> p (g b u)").bitcast(BF16),
+                )
+                x_codes[(w, h)], x_scales[(w, h)] = codes, scales
+
+        def first_matmul(n):
+            w, j = regions[n]
+            u = psum_u.tile([P, F], F32)
+            for c in range(W1_PASSES):
+                h = image_row(j, c // ROW_PASSES)
+                g = c % ROW_PASSES
+                nc.tensor.matmul_mx(
+                    out=u[:],
+                    lhsT=x_codes[(w, h)][:, g, :].bitcast(FP8X4),
+                    lhsT_scale=x_scales[(w, h)][:, g, :],
+                    rhs=w1_codes[:, c, :].bitcast(FP8X4),
+                    rhs_scale=w1_scales[:, c, :],
+                    start=(c == 0),
+                    stop=(c == W1_PASSES - 1),
+                )
+            u_bank[n] = u
+
+        def statistics(n):
+            stats = work.tile([P, 6], F32)
+            nc.vector.bn_stats(out=stats[:], in_=u_bank[n][:])
+            mv = work.tile([P, 2], F32)
+            nc.vector.bn_aggr(out=mv[:], in_=stats[:])
+            mean_var[n] = mv
+
+        def normalise(n):
+            mv = mean_var[n]
+            rstd = work.tile([P, 1], F32)
+            nc.scalar.activation(
+                out=rstd[:], in_=mv[:, 1:2], func=ACT.Abs_reciprocal_sqrt, bias=eps[:]
+            )
+            shift = work.tile([P, 1], F32)
+            nc.scalar.activation(out=shift[:], in_=mv[:, 0:1], func=ACT.Copy, scale=rstd[:])
+            nc.scalar.mul(out=shift[:], in_=shift[:], mul=-1.0)
+            norm = work.tile([P, F], F32)
+            nc.scalar.activation(
+                out=norm[:].rearrange("p (t m) -> p t m", t=PACK),
+                in_=u_bank[n][:].rearrange("p (m t) -> p t m", t=PACK),
+                func=ACT.Identity, scale=rstd[:], bias=shift[:],
+            )
+            norms[n] = norm
+
+        def transpose_hidden(n):
+            hid_t = psum_h.tile([P, PACK, P], F32, tag="hid_t")
+            for t in range(PACK):
+                nc.tensor.transpose(hid_t[:, t, :], norms[n][:, t * P : (t + 1) * P], ident[:])
+            hid_ts[n] = hid_t
+
+        def activate_hidden(n):
+            planes = work.tile([P, PACK, P], BF16)
+            for t in range(PACK):
+                nc.scalar.activation(
+                    out=planes[:, t, :], in_=hid_ts[n][:, t, :], func=ACT.Relu,
+                    scale=gain_cols[:, t : t + 1], bias=gain_cols[:, PACK + t : PACK + t + 1],
+                )
+            hid_planes[n] = planes
+
+        def quantise_hidden(n):
+            grouped = work.tile([P, P, PACK], BF16, align_bytes=64, tag="hid_grouped")
+            nc.vector.tensor_copy(
+                out=grouped[:].rearrange("p (c i) t -> p c t i", i=4),
+                in_=hid_planes[n][:].rearrange("p t (c i) -> p c t i", i=4),
+            )
+            codes = work.tile([P, P], U32, align_bytes=64, tag="hid_codes")
+            scales = work.tile([P, P], U8, align_bytes=64, tag="hid_scales")
+            nc.vector.quantize_mx(
+                out=codes[:].bitcast(FP8X4),
+                scales=scales[:],
+                in_=grouped[:].rearrange("p b t -> p (b t)"),
+            )
+            hid_codes[n], hid_scales[n] = codes, scales
+
+        def second_matmul(n):
+            w, j = regions[n]
+            for pixel in range(PIXEL):
+                if j == 0 and pixel == 0:
+                    continue
+                result = out_pool.tile([P, C], F32)
+                for half in range(ROW_BLOCKS):
+                    block = pixel * ROW_BLOCKS + half
+                    y = psum_y.tile([P, N_TILE], F32)
+                    nc.tensor.matmul_mx(
+                        out=y[:],
+                        lhsT=hid_codes[n][:].bitcast(FP8X4),
+                        lhsT_scale=hid_scales[n][:],
+                        rhs=w2_codes[:, block, :].bitcast(FP8X4),
+                        rhs_scale=w2_scales[:, block, :],
+                        start=True,
+                        stop=True,
+                    )
+                    nc.vector.tensor_tensor(
+                        out=result[:, half * N_TILE : (half + 1) * N_TILE],
+                        in0=y[:],
+                        in1=bias2[:, block * N_TILE : (block + 1) * N_TILE],
+                        op=ALU.add,
+                    )
+                nc.sync.dma_start(out=out[:, image_row(j, pixel), w, :], in_=result[:])
+
+        def run(stage_of_region, n):
+            if 0 <= n < len(regions):
+                stage_of_region(n)
+
+        w2_grouped = {}
+        for step in range(len(regions) + 5):
+            run(transpose_x, step)
+            run(quantise_hidden, step - 4)
+            run(copy_x, step)
+            run(quantise_x, step)
+            run(first_matmul, step - 1)
+            run(statistics, step - 1)
+            if 1 <= step <= W2_BLOCKS:
+                n = w2_order[step - 1]
+                quantise_weight_block(w2_grouped[n], w2_codes[:, n, :], w2_scales[:, n, :])
+            run(normalise, step - 2)
+            run(transpose_hidden, step - 3)
+            if step < W2_BLOCKS:
+                n = w2_order[step]
+                w2_grouped[n] = regroup_weight_block(w2_raw[:, n])
+            run(activate_hidden, step - 3)
+            run(second_matmul, step - 5)

@@ -46,9 +46,9 @@ def tile_hiremodule_pa_kernel(tc, x, wh1, gh, bh, wh2, bh2, out):
         x_code_pool = ctx.enter_context(tc.tile_pool(name="x_code_pool", bufs=2 * H))
         out_pool = ctx.enter_context(tc.tile_pool(name="out_pool", bufs=6))
         psum_x = ctx.enter_context(tc.psum_pool(name="psum_x", bufs=2))
-        psum_u = ctx.enter_context(tc.psum_pool(name="psum_u", bufs=2))
+        psum_u = ctx.enter_context(tc.psum_pool(name="psum_u", bufs=1))
         psum_h = ctx.enter_context(tc.psum_pool(name="psum_h", bufs=1))
-        psum_y = ctx.enter_context(tc.psum_pool(name="psum_y", bufs=3))
+        psum_y = ctx.enter_context(tc.psum_pool(name="psum_y", bufs=4))
 
         def new_rows(j):
             rows = [image_row(j, pixel) for pixel in range(PIXEL)]
@@ -96,6 +96,8 @@ def tile_hiremodule_pa_kernel(tc, x, wh1, gh, bh, wh2, bh2, out):
         make_identity(nc, ident[:])
         eps = consts.tile([P, 1], F32)
         nc.vector.memset(eps[:], EPS)
+        warm = consts.tile([P, 1], F32)
+        nc.scalar.activation(out=warm[:], in_=eps[:], func=ACT.Abs_reciprocal_sqrt, bias=eps[:])
 
         gain_cols = consts.tile([P, 2 * PACK], F32)
         nc.vector.tensor_copy(out=gain_cols[:, 0:PACK], in_=gain_raw[:])
@@ -111,6 +113,14 @@ def tile_hiremodule_pa_kernel(tc, x, wh1, gh, bh, wh2, bh2, out):
             nc.scalar.copy(
                 out=grouped[:, half:, :].rearrange("p (c i) t -> p c t i", i=4),
                 in_=raw[:, :, half:].rearrange("p t (c i) -> p c t i", i=4),
+            )
+            return grouped
+
+        def regroup_weight_block_on_gpsimd(raw):
+            grouped = stage.tile([P, N_TILE, PACK], BF16, align_bytes=64, tag="w2_grouped")
+            nc.gpsimd.tensor_scalar(
+                out=grouped[:], in0=raw.rearrange("p t c -> p c t"),
+                scalar1=1.0, scalar2=0.0, op0=ALU.mult, op1=ALU.add,
             )
             return grouped
 
@@ -133,7 +143,8 @@ def tile_hiremodule_pa_kernel(tc, x, wh1, gh, bh, wh2, bh2, out):
         w2_scales = consts.tile([P, W2_BLOCKS, N_TILE], U8, align_bytes=64)
 
         x_t, x_grouped, x_codes, x_scales = {}, {}, {}, {}
-        u_bank, mean_var, norms, hid_ts, hid_planes, hid_codes, hid_scales = {}, {}, {}, {}, {}, {}, {}
+        u_bank, u_rows, totals, shifts, square_sums, rstds, norms = {}, {}, {}, {}, {}, {}, {}
+        hid_ts, hid_planes, hid_grouped, hid_codes, hid_scales = {}, {}, {}, {}, {}
 
         def transpose_x(n):
             w, j = regions[n]
@@ -185,27 +196,43 @@ def tile_hiremodule_pa_kernel(tc, x, wh1, gh, bh, wh2, bh2, out):
                 )
             u_bank[n] = u
 
-        def statistics(n):
-            stats = work.tile([P, 6], F32)
-            nc.vector.bn_stats(out=stats[:], in_=u_bank[n][:])
-            mv = work.tile([P, 2], F32)
-            nc.vector.bn_aggr(out=mv[:], in_=stats[:])
-            mean_var[n] = mv
+        def copy_u(n):
+            u_row = work.tile([P, F], F32)
+            total = work.tile([P, 1], F32)
+            nc.scalar.activation(
+                out=u_row[:].rearrange("p (t m) -> p t m", t=PACK),
+                in_=u_bank[n][:].rearrange("p (m t) -> p t m", t=PACK),
+                func=ACT.Identity, accum_out=total[:],
+            )
+            u_rows[n], totals[n] = u_row, total
 
-        def normalise(n):
-            mv = mean_var[n]
+        def minus_mean(n):
+            shift = work.tile([P, 1], F32)
+            nc.scalar.mul(out=shift[:], in_=totals[n][:], mul=-1.0 / F)
+            shifts[n] = shift
+
+        def spread(n):
+            squares = work.tile([P, F], BF16)
+            square_sum = work.tile([P, 1], F32)
+            nc.scalar.activation(
+                out=squares[:], in_=u_rows[n][:], func=ACT.Square, bias=shifts[n][:],
+                accum_out=square_sum[:],
+            )
+            square_sums[n] = square_sum
+
+        def reciprocal_std(n):
             rstd = work.tile([P, 1], F32)
             nc.scalar.activation(
-                out=rstd[:], in_=mv[:, 1:2], func=ACT.Abs_reciprocal_sqrt, bias=eps[:]
+                out=rstd[:], in_=square_sums[n][:], func=ACT.Abs_reciprocal_sqrt,
+                scale=1.0 / F, bias=eps[:],
             )
-            shift = work.tile([P, 1], F32)
-            nc.scalar.activation(out=shift[:], in_=mv[:, 0:1], func=ACT.Copy, scale=rstd[:])
-            nc.scalar.mul(out=shift[:], in_=shift[:], mul=-1.0)
+            rstds[n] = rstd
+
+        def normalise(n):
             norm = work.tile([P, F], F32)
-            nc.scalar.activation(
-                out=norm[:].rearrange("p (t m) -> p t m", t=PACK),
-                in_=u_bank[n][:].rearrange("p (m t) -> p t m", t=PACK),
-                func=ACT.Identity, scale=rstd[:], bias=shift[:],
+            nc.vector.tensor_scalar(
+                out=norm[:], in0=u_rows[n][:], scalar1=shifts[n][:], scalar2=rstds[n][:],
+                op0=ALU.add, op1=ALU.mult,
             )
             norms[n] = norm
 
@@ -224,18 +251,21 @@ def tile_hiremodule_pa_kernel(tc, x, wh1, gh, bh, wh2, bh2, out):
                 )
             hid_planes[n] = planes
 
-        def quantise_hidden(n):
+        def regroup_hidden(n):
             grouped = work.tile([P, P, PACK], BF16, align_bytes=64, tag="hid_grouped")
             nc.vector.tensor_copy(
                 out=grouped[:].rearrange("p (c i) t -> p c t i", i=4),
                 in_=hid_planes[n][:].rearrange("p t (c i) -> p c t i", i=4),
             )
+            hid_grouped[n] = grouped
+
+        def quantise_hidden(n):
             codes = work.tile([P, P], U32, align_bytes=64, tag="hid_codes")
             scales = work.tile([P, P], U8, align_bytes=64, tag="hid_scales")
             nc.vector.quantize_mx(
                 out=codes[:].bitcast(FP8X4),
                 scales=scales[:],
-                in_=grouped[:].rearrange("p b t -> p (b t)"),
+                in_=hid_grouped[n][:].rearrange("p b t -> p (b t)"),
             )
             hid_codes[n], hid_scales[n] = codes, scales
 
@@ -270,20 +300,24 @@ def tile_hiremodule_pa_kernel(tc, x, wh1, gh, bh, wh2, bh2, out):
                 stage_of_region(n)
 
         w2_grouped = {}
-        for step in range(len(regions) + 5):
+        for step in range(len(regions) + 4):
             run(transpose_x, step)
-            run(quantise_hidden, step - 4)
+            run(transpose_hidden, step - 3)
+            run(copy_u, step - 2)
             run(copy_x, step)
+            run(minus_mean, step - 2)
             run(quantise_x, step)
+            run(activate_hidden, step - 3)
+            run(spread, step - 2)
+            run(reciprocal_std, step - 2)
             run(first_matmul, step - 1)
-            run(statistics, step - 1)
+            run(regroup_hidden, step - 3)
+            run(normalise, step - 2)
+            run(quantise_hidden, step - 3)
             if 1 <= step <= W2_BLOCKS:
                 n = w2_order[step - 1]
                 quantise_weight_block(w2_grouped[n], w2_codes[:, n, :], w2_scales[:, n, :])
-            run(normalise, step - 2)
-            run(transpose_hidden, step - 3)
+            run(second_matmul, step - 4)
             if step < W2_BLOCKS:
                 n = w2_order[step]
-                w2_grouped[n] = regroup_weight_block(w2_raw[:, n])
-            run(activate_hidden, step - 3)
-            run(second_matmul, step - 5)
+                w2_grouped[n] = regroup_weight_block_on_gpsimd(w2_raw[:, n])

@@ -116,11 +116,11 @@ def tile_hiremodule_pa_kernel(tc, x, wh1, gh, bh, wh2, bh2, out):
             )
             return grouped
 
-        def regroup_weight_block_on_gpsimd(raw):
+        def regroup_weight_block_on_vector(raw):
             grouped = stage.tile([P, N_TILE, PACK], BF16, align_bytes=64, tag="w2_grouped")
-            nc.gpsimd.tensor_scalar(
-                out=grouped[:], in0=raw.rearrange("p t c -> p c t"),
-                scalar1=1.0, scalar2=0.0, op0=ALU.mult, op1=ALU.add,
+            nc.vector.tensor_copy(
+                out=grouped[:].rearrange("p (c i) t -> p c t i", i=4),
+                in_=raw.rearrange("p t (c i) -> p c t i", i=4),
             )
             return grouped
 
@@ -320,4 +320,4 @@ def tile_hiremodule_pa_kernel(tc, x, wh1, gh, bh, wh2, bh2, out):
             run(second_matmul, step - 4)
             if step < W2_BLOCKS:
                 n = w2_order[step]
-                w2_grouped[n] = regroup_weight_block_on_gpsimd(w2_raw[:, n])
+                w2_grouped[n] = regroup_weight_block_on_vector(w2_raw[:, n])

@@ -40,7 +40,8 @@ def tile_hiremodule_pa_kernel(tc, x, wh1, gh, bh, wh2, bh2, out):
     with ExitStack() as ctx:
         ctx.enter_context(tc.manual_schedule())
         consts = ctx.enter_context(tc.tile_pool(name="consts", bufs=1))
-        x_pool = ctx.enter_context(tc.tile_pool(name="x_pool", bufs=H * W))
+        x_pool = ctx.enter_context(tc.tile_pool(name="x_pool", bufs=H))
+        x_column_pool = ctx.enter_context(tc.tile_pool(name="x_column_pool", bufs=W - 1))
         stage = ctx.enter_context(tc.tile_pool(name="stage", bufs=3))
         work = ctx.enter_context(tc.tile_pool(name="work", bufs=3))
         x_code_pool = ctx.enter_context(tc.tile_pool(name="x_code_pool", bufs=2 * H))
@@ -57,16 +58,22 @@ def tile_hiremodule_pa_kernel(tc, x, wh1, gh, bh, wh2, bh2, out):
         x_rows = {}
 
         def load_x(w):
-            for j in range(R):
-                for h in new_rows(j):
-                    x_row = x_pool.tile([P, C], BF16)
-                    nc.sync.dma_start(out=x_row[:], in_=x[:, h, w, :])
-                    x_rows[(w, h)] = x_row
+            if w == 0:
+                for j in range(R):
+                    for h in new_rows(j):
+                        x_row = x_pool.tile([P, C], BF16)
+                        nc.sync.dma_start(out=x_row[:], in_=x[:, h, w, :])
+                        x_rows[(w, h)] = x_row[:]
+            else:
+                x_column = x_column_pool.tile([P, H, C], BF16)
+                nc.sync.dma_start(out=x_column[:], in_=x[:, :, w, :])
+                for h in range(H):
+                    x_rows[(w, h)] = x_column[:, h, :]
 
         gain_raw = consts.tile([P, PACK], BF16)
-        nc.sync.dma_start(out=gain_raw[:], in_=gh.rearrange("(p t) -> p t", t=PACK))
+        nc.scalar.dma_start(out=gain_raw[:], in_=gh.rearrange("(p t) -> p t", t=PACK))
         shift_raw = consts.tile([P, PACK], BF16)
-        nc.sync.dma_start(out=shift_raw[:], in_=bh.rearrange("(p t) -> p t", t=PACK))
+        nc.scalar.dma_start(out=shift_raw[:], in_=bh.rearrange("(p t) -> p t", t=PACK))
         w1_raw = consts.tile([P, W1_PASSES, PACK, F], BF16)
         for c in range(W1_PASSES):
             nc.sync.dma_start(
@@ -98,10 +105,6 @@ def tile_hiremodule_pa_kernel(tc, x, wh1, gh, bh, wh2, bh2, out):
         nc.vector.memset(eps[:], EPS)
         warm = consts.tile([P, 1], F32)
         nc.scalar.activation(out=warm[:], in_=eps[:], func=ACT.Abs_reciprocal_sqrt, bias=eps[:])
-
-        gain_cols = consts.tile([P, 2 * PACK], F32)
-        nc.vector.tensor_copy(out=gain_cols[:, 0:PACK], in_=gain_raw[:])
-        nc.vector.tensor_copy(out=gain_cols[:, PACK : 2 * PACK], in_=shift_raw[:])
 
         def regroup_weight_block(raw):
             grouped = stage.tile([P, N_TILE, PACK], BF16, align_bytes=64, tag="w_grouped")
@@ -142,14 +145,19 @@ def tile_hiremodule_pa_kernel(tc, x, wh1, gh, bh, wh2, bh2, out):
         w2_codes = consts.tile([P, W2_BLOCKS, N_TILE], U32, align_bytes=64)
         w2_scales = consts.tile([P, W2_BLOCKS, N_TILE], U8, align_bytes=64)
 
+        gain_cols = consts.tile([P, 2 * PACK], F32)
+        nc.vector.tensor_copy(out=gain_cols[:, 0:PACK], in_=gain_raw[:])
+        nc.vector.tensor_copy(out=gain_cols[:, PACK : 2 * PACK], in_=shift_raw[:])
+
         x_t, x_grouped, x_codes, x_scales = {}, {}, {}, {}
         u_bank, u_rows, totals, shifts, square_sums, rstds, norms = {}, {}, {}, {}, {}, {}, {}
         hid_ts, hid_planes, hid_grouped, hid_codes, hid_scales = {}, {}, {}, {}, {}
+        y_bank, results = {}, {}
 
         def transpose_x(n):
             w, j = regions[n]
             for h in new_rows(j):
-                x_words = x_rows[(w, h)][:].bitcast(F32)
+                x_words = x_rows[(w, h)].bitcast(F32)
                 bank = psum_x.tile([P, 2 * ROW_PASSES, P], F32)
                 for q in range(2 * ROW_PASSES):
                     first = (q // 2) * 2 * P + q % 2
@@ -269,31 +277,48 @@ def tile_hiremodule_pa_kernel(tc, x, wh1, gh, bh, wh2, bh2, out):
             )
             hid_codes[n], hid_scales[n] = codes, scales
 
+        def banks(n):
+            first_pixel = 1 if regions[n][1] == 0 else 0
+            return [(pixel, half) for pixel in range(first_pixel, PIXEL) for half in range(ROW_BLOCKS)]
+
         def second_matmul(n):
+            for pixel, half in banks(n):
+                block = pixel * ROW_BLOCKS + half
+                y = psum_y.tile([P, N_TILE], F32)
+                nc.tensor.matmul_mx(
+                    out=y[:],
+                    lhsT=hid_codes[n][:].bitcast(FP8X4),
+                    lhsT_scale=hid_scales[n][:],
+                    rhs=w2_codes[:, block, :].bitcast(FP8X4),
+                    rhs_scale=w2_scales[:, block, :],
+                    start=True,
+                    stop=True,
+                )
+                y_bank[(n, pixel, half)] = y
+
+        def add_bias(n, some_banks):
             w, j = regions[n]
-            for pixel in range(PIXEL):
-                if j == 0 and pixel == 0:
-                    continue
-                result = out_pool.tile([P, C], F32)
-                for half in range(ROW_BLOCKS):
-                    block = pixel * ROW_BLOCKS + half
-                    y = psum_y.tile([P, N_TILE], F32)
-                    nc.tensor.matmul_mx(
-                        out=y[:],
-                        lhsT=hid_codes[n][:].bitcast(FP8X4),
-                        lhsT_scale=hid_scales[n][:],
-                        rhs=w2_codes[:, block, :].bitcast(FP8X4),
-                        rhs_scale=w2_scales[:, block, :],
-                        start=True,
-                        stop=True,
+            for pixel, half in some_banks:
+                block = pixel * ROW_BLOCKS + half
+                if half == 0:
+                    result = out_pool.tile([P, C], F32)
+                    results[(n, pixel)] = result
+                nc.vector.tensor_tensor(
+                    out=results[(n, pixel)][:, half * N_TILE : (half + 1) * N_TILE],
+                    in0=y_bank[(n, pixel, half)][:],
+                    in1=bias2[:, block * N_TILE : (block + 1) * N_TILE],
+                    op=ALU.add,
+                )
+                if half == ROW_BLOCKS - 1:
+                    nc.sync.dma_start(
+                        out=out[:, image_row(j, pixel), w, :], in_=results[(n, pixel)][:]
                     )
-                    nc.vector.tensor_tensor(
-                        out=result[:, half * N_TILE : (half + 1) * N_TILE],
-                        in0=y[:],
-                        in1=bias2[:, block * N_TILE : (block + 1) * N_TILE],
-                        op=ALU.add,
-                    )
-                nc.sync.dma_start(out=out[:, image_row(j, pixel), w, :], in_=result[:])
+
+        def add_first_bias(n):
+            add_bias(n, banks(n)[:1])
+
+        def add_other_biases(n):
+            add_bias(n, banks(n)[1:])
 
         def run(stage_of_region, n):
             if 0 <= n < len(regions):
@@ -304,20 +329,22 @@ def tile_hiremodule_pa_kernel(tc, x, wh1, gh, bh, wh2, bh2, out):
             run(transpose_x, step)
             run(transpose_hidden, step - 3)
             run(copy_u, step - 2)
-            run(copy_x, step)
             run(minus_mean, step - 2)
+            run(spread, step - 2)
+            run(first_matmul, step - 1)
+            run(copy_x, step)
+            run(reciprocal_std, step - 2)
+            run(normalise, step - 2)
             run(quantise_x, step)
             run(activate_hidden, step - 3)
-            run(spread, step - 2)
-            run(reciprocal_std, step - 2)
-            run(first_matmul, step - 1)
+            run(second_matmul, step - 4)
             run(regroup_hidden, step - 3)
-            run(normalise, step - 2)
+            run(add_first_bias, step - 4)
             run(quantise_hidden, step - 3)
             if 1 <= step <= W2_BLOCKS:
                 n = w2_order[step - 1]
                 quantise_weight_block(w2_grouped[n], w2_codes[:, n, :], w2_scales[:, n, :])
-            run(second_matmul, step - 4)
+            run(add_other_biases, step - 4)
             if step < W2_BLOCKS:
                 n = w2_order[step]
                 w2_grouped[n] = regroup_weight_block_on_vector(w2_raw[:, n])

@@ -57,30 +57,36 @@ def tile_hiremodule_pa_kernel(tc, x, wh1, gh, bh, wh2, bh2, out):
 
         x_rows = {}
 
-        def load_x(w):
-            if w == 0:
-                for j in range(R):
-                    for h in new_rows(j):
-                        x_row = x_pool.tile([P, C], BF16)
-                        nc.sync.dma_start(out=x_row[:], in_=x[:, h, w, :])
-                        x_rows[(w, h)] = x_row[:]
-            else:
-                x_column = x_column_pool.tile([P, H, C], BF16)
-                nc.sync.dma_start(out=x_column[:], in_=x[:, :, w, :])
-                for h in range(H):
-                    x_rows[(w, h)] = x_column[:, h, :]
+        def load_x_rows(j):
+            for h in new_rows(j):
+                x_row = x_pool.tile([P, C], BF16)
+                nc.sync.dma_start(out=x_row[:], in_=x[:, h, 0, :])
+                x_rows[(0, h)] = x_row[:]
+
+        def load_x_column(w):
+            x_column = x_column_pool.tile([P, H, C], BF16)
+            nc.sync.dma_start(out=x_column[:], in_=x[:, :, w, :])
+            for h in range(H):
+                x_rows[(w, h)] = x_column[:, h, :]
 
         gain_raw = consts.tile([P, PACK], BF16)
         nc.scalar.dma_start(out=gain_raw[:], in_=gh.rearrange("(p t) -> p t", t=PACK))
         shift_raw = consts.tile([P, PACK], BF16)
         nc.scalar.dma_start(out=shift_raw[:], in_=bh.rearrange("(p t) -> p t", t=PACK))
         w1_raw = consts.tile([P, W1_PASSES, PACK, F], BF16)
-        for c in range(W1_PASSES):
-            nc.sync.dma_start(
-                out=w1_raw[:, c],
-                in_=wh1[c * K_PASS : (c + 1) * K_PASS, :].rearrange("(p t) f -> p t f", t=PACK),
-            )
-        load_x(0)
+
+        def load_w1(passes):
+            for c in passes:
+                nc.sync.dma_start(
+                    out=w1_raw[:, c],
+                    in_=wh1[c * K_PASS : (c + 1) * K_PASS, :].rearrange("(p t) f -> p t f", t=PACK),
+                )
+
+        load_w1(range(W1_PASSES // 2))
+        load_x_rows(0)
+        load_w1(range(W1_PASSES // 2, W1_PASSES))
+        for j in range(1, R):
+            load_x_rows(j)
         w2_order = [(k + W2_BLOCKS // 2) % W2_BLOCKS for k in range(W2_BLOCKS)]
         w2_raw = consts.tile([P, W2_BLOCKS, PACK, N_TILE], BF16)
 
@@ -92,12 +98,12 @@ def tile_hiremodule_pa_kernel(tc, x, wh1, gh, bh, wh2, bh2, out):
                 )
 
         load_w2(w2_order[: W2_BLOCKS // 2])
-        load_x(1)
+        load_x_column(1)
         load_w2(w2_order[W2_BLOCKS // 2 :])
         bias2 = consts.tile([P, K1], BF16)
         nc.sync.dma_start(out=bias2[:], in_=bh2.partition_broadcast(P))
         for w in range(2, W):
-            load_x(w)
+            load_x_column(w)
 
         ident = consts.tile([P, P], F32)
         make_identity(nc, ident[:])
@@ -136,18 +142,8 @@ def tile_hiremodule_pa_kernel(tc, x, wh1, gh, bh, wh2, bh2, out):
 
         w1_codes = consts.tile([P, W1_PASSES, F], U32, align_bytes=64)
         w1_scales = consts.tile([P, W1_PASSES, F], U8, align_bytes=64)
-        w1_grouped = {}
-        for c in range(W1_PASSES + 1):
-            if c < W1_PASSES:
-                w1_grouped[c] = regroup_weight_block(w1_raw[:, c])
-            if c > 0:
-                quantise_weight_block(w1_grouped[c - 1], w1_codes[:, c - 1, :], w1_scales[:, c - 1, :])
         w2_codes = consts.tile([P, W2_BLOCKS, N_TILE], U32, align_bytes=64)
         w2_scales = consts.tile([P, W2_BLOCKS, N_TILE], U8, align_bytes=64)
-
-        gain_cols = consts.tile([P, 2 * PACK], F32)
-        nc.vector.tensor_copy(out=gain_cols[:, 0:PACK], in_=gain_raw[:])
-        nc.vector.tensor_copy(out=gain_cols[:, PACK : 2 * PACK], in_=shift_raw[:])
 
         x_t, x_grouped, x_codes, x_scales = {}, {}, {}, {}
         u_bank, u_rows, totals, shifts, square_sums, rstds, norms = {}, {}, {}, {}, {}, {}, {}
@@ -324,8 +320,28 @@ def tile_hiremodule_pa_kernel(tc, x, wh1, gh, bh, wh2, bh2, out):
             if 0 <= n < len(regions):
                 stage_of_region(n)
 
-        w2_grouped = {}
-        for step in range(len(regions) + 4):
+        def keep_tensor_busy(rows):
+            y = psum_y.tile([P, N_TILE], F32)
+            for repeat in range(2):
+                nc.tensor.matmul(y[:], lhsT=rows[:, :P], rhs=rows, start=True, stop=True)
+
+        w1_grouped = {}
+        for c in range(W1_PASSES + 1):
+            if c < W1_PASSES:
+                w1_grouped[c] = regroup_weight_block(w1_raw[:, c])
+                keep_tensor_busy(w1_raw[:, c, 0, :])
+            if c > 0:
+                quantise_weight_block(w1_grouped[c - 1], w1_codes[:, c - 1, :], w1_scales[:, c - 1, :])
+            if c == W1_PASSES // 2 - 1:
+                run(transpose_x, 0)
+                run(copy_x, 0)
+            if c == W1_PASSES // 2:
+                run(quantise_x, 0)
+        gain_cols = consts.tile([P, 2 * PACK], F32)
+        nc.vector.tensor_copy(out=gain_cols[:, 0:PACK], in_=gain_raw[:])
+        nc.vector.tensor_copy(out=gain_cols[:, PACK : 2 * PACK], in_=shift_raw[:])
+        w2_grouped = {w2_order[0]: regroup_weight_block_on_vector(w2_raw[:, w2_order[0]])}
+        for step in range(1, len(regions) + 4):
             run(transpose_x, step)
             run(transpose_hidden, step - 3)
             run(copy_u, step - 2)

@@ -36,12 +36,12 @@ def image_row(j, pixel):
 
 def tile_hiremodule_pa_kernel(tc, x, wh1, gh, bh, wh2, bh2, out):
     nc = tc.nc
-    regions = [(w, j) for w in range(W) for j in range(R)]
+    region_order = [[0, 1, 2]] * (W - 1) + [[1, 2, 0]]
+    regions = [(w, j) for w in range(W) for j in region_order[w]]
     with ExitStack() as ctx:
         ctx.enter_context(tc.manual_schedule())
         consts = ctx.enter_context(tc.tile_pool(name="consts", bufs=1))
-        x_pool = ctx.enter_context(tc.tile_pool(name="x_pool", bufs=H))
-        x_column_pool = ctx.enter_context(tc.tile_pool(name="x_column_pool", bufs=W - 1))
+        x_pool = ctx.enter_context(tc.tile_pool(name="x_pool", bufs=1))
         stage = ctx.enter_context(tc.tile_pool(name="stage", bufs=3))
         work = ctx.enter_context(tc.tile_pool(name="work", bufs=3))
         x_code_pool = ctx.enter_context(tc.tile_pool(name="x_code_pool", bufs=2 * H))
@@ -51,23 +51,23 @@ def tile_hiremodule_pa_kernel(tc, x, wh1, gh, bh, wh2, bh2, out):
         psum_h = ctx.enter_context(tc.psum_pool(name="psum_h", bufs=1))
         psum_y = ctx.enter_context(tc.psum_pool(name="psum_y", bufs=4))
 
-        def new_rows(j):
+        def new_rows(w, j):
+            earlier = region_order[w][: region_order[w].index(j)]
+            read = [image_row(i, pixel) for i in earlier for pixel in range(PIXEL)]
             rows = [image_row(j, pixel) for pixel in range(PIXEL)]
-            return [h for h in rows if j == 0 or h != image_row(0, 0)]
+            return [h for h in rows if h not in read]
 
         x_rows = {}
 
-        def load_x_rows(j):
-            for h in new_rows(j):
-                x_row = x_pool.tile([P, C], BF16)
-                nc.sync.dma_start(out=x_row[:], in_=x[:, h, 0, :])
-                x_rows[(0, h)] = x_row[:]
+        def load_x(w, rows):
+            step = rows[1] - rows[0] if len(rows) > 1 else 1
+            x_part = x_pool.tile([P, len(rows), C], BF16, tag="x_%d_%d" % (w, rows[0]))
+            nc.sync.dma_start(out=x_part[:], in_=x[:, rows[0] : rows[-1] + 1 : step, w, :])
+            for i, h in enumerate(rows):
+                x_rows[(w, h)] = x_part[:, i, :]
 
-        def load_x_column(w):
-            x_column = x_column_pool.tile([P, H, C], BF16)
-            nc.sync.dma_start(out=x_column[:], in_=x[:, :, w, :])
-            for h in range(H):
-                x_rows[(w, h)] = x_column[:, h, :]
+        def load_region(w, j):
+            load_x(w, sorted(new_rows(w, j)))
 
         gain_raw = consts.tile([P, PACK], BF16)
         nc.scalar.dma_start(out=gain_raw[:], in_=gh.rearrange("(p t) -> p t", t=PACK))
@@ -83,27 +83,25 @@ def tile_hiremodule_pa_kernel(tc, x, wh1, gh, bh, wh2, bh2, out):
                 )
 
         load_w1(range(W1_PASSES // 2))
-        load_x_rows(0)
+        for h in new_rows(0, 0):
+            load_x(0, [h])
         load_w1(range(W1_PASSES // 2, W1_PASSES))
-        for j in range(1, R):
-            load_x_rows(j)
+        load_region(0, 1)
+        load_region(0, 2)
         w2_order = [(k + W2_BLOCKS // 2) % W2_BLOCKS for k in range(W2_BLOCKS)]
         w2_raw = consts.tile([P, W2_BLOCKS, PACK, N_TILE], BF16)
-
-        def load_w2(blocks):
-            for n in blocks:
-                nc.sync.dma_start(
-                    out=w2_raw[:, n],
-                    in_=wh2[:, n * N_TILE : (n + 1) * N_TILE].rearrange("(p t) c -> p t c", t=PACK),
-                )
-
-        load_w2(w2_order[: W2_BLOCKS // 2])
-        load_x_column(1)
-        load_w2(w2_order[W2_BLOCKS // 2 :])
+        for n, (w, j) in zip(w2_order, [(1, 0), (1, 1), (1, 2), (2, 0)]):
+            nc.sync.dma_start(
+                out=w2_raw[:, n],
+                in_=wh2[:, n * N_TILE : (n + 1) * N_TILE].rearrange("(p t) c -> p t c", t=PACK),
+            )
+            load_region(w, j)
         bias2 = consts.tile([P, K1], BF16)
         nc.sync.dma_start(out=bias2[:], in_=bh2.partition_broadcast(P))
-        for w in range(2, W):
-            load_x_column(w)
+        load_region(2, 1)
+        load_region(2, 2)
+        for w in range(3, W):
+            load_x(w, list(range(H)))
 
         ident = consts.tile([P, P], F32)
         make_identity(nc, ident[:])
@@ -152,7 +150,7 @@ def tile_hiremodule_pa_kernel(tc, x, wh1, gh, bh, wh2, bh2, out):
 
         def transpose_x(n):
             w, j = regions[n]
-            for h in new_rows(j):
+            for h in new_rows(w, j):
                 x_words = x_rows[(w, h)].bitcast(F32)
                 bank = psum_x.tile([P, 2 * ROW_PASSES, P], F32)
                 for q in range(2 * ROW_PASSES):
@@ -164,7 +162,7 @@ def tile_hiremodule_pa_kernel(tc, x, wh1, gh, bh, wh2, bh2, out):
 
         def copy_x(n):
             w, j = regions[n]
-            for h in new_rows(j):
+            for h in new_rows(w, j):
                 grouped = stage.tile([P, ROW_PASSES, P, 2], F32, align_bytes=64, tag="x_grouped")
                 nc.scalar.copy(
                     out=grouped[:], in_=x_t[(w, h)][:].rearrange("p (g u) b -> p g b u", u=2)
@@ -173,7 +171,7 @@ def tile_hiremodule_pa_kernel(tc, x, wh1, gh, bh, wh2, bh2, out):
 
         def quantise_x(n):
             w, j = regions[n]
-            for h in new_rows(j):
+            for h in new_rows(w, j):
                 codes = x_code_pool.tile([P, ROW_PASSES, P], U32, align_bytes=64, tag="x_codes")
                 scales = x_code_pool.tile([P, ROW_PASSES, P], U8, align_bytes=64, tag="x_scales")
                 nc.vector.quantize_mx(
@@ -299,16 +297,18 @@ def tile_hiremodule_pa_kernel(tc, x, wh1, gh, bh, wh2, bh2, out):
                 if half == 0:
                     result = out_pool.tile([P, C], F32)
                     results[(n, pixel)] = result
+                columns = results[(n, pixel)][:, half * N_TILE : (half + 1) * N_TILE]
                 nc.vector.tensor_tensor(
-                    out=results[(n, pixel)][:, half * N_TILE : (half + 1) * N_TILE],
+                    out=columns,
                     in0=y_bank[(n, pixel, half)][:],
                     in1=bias2[:, block * N_TILE : (block + 1) * N_TILE],
                     op=ALU.add,
                 )
-                if half == ROW_BLOCKS - 1:
-                    nc.sync.dma_start(
-                        out=out[:, image_row(j, pixel), w, :], in_=results[(n, pixel)][:]
-                    )
+                row = out[:, image_row(j, pixel), w, :]
+                if n == len(regions) - 1:
+                    nc.sync.dma_start(out=row[:, half * N_TILE : (half + 1) * N_TILE], in_=columns)
+                elif half == ROW_BLOCKS - 1:
+                    nc.sync.dma_start(out=row, in_=results[(n, pixel)][:])
 
         def add_first_bias(n):
             add_bias(n, banks(n)[:1])

@@ -341,26 +341,26 @@ def tile_hiremodule_pa_kernel(tc, x, wh1, gh, bh, wh2, bh2, out):
         nc.vector.tensor_copy(out=gain_cols[:, 0:PACK], in_=gain_raw[:])
         nc.vector.tensor_copy(out=gain_cols[:, PACK : 2 * PACK], in_=shift_raw[:])
         w2_grouped = {w2_order[0]: regroup_weight_block_on_vector(w2_raw[:, w2_order[0]])}
-        for step in range(1, len(regions) + 4):
+        for step in range(1, len(regions) + 5):
             run(transpose_x, step)
-            run(transpose_hidden, step - 3)
+            run(transpose_hidden, step - 4)
             run(copy_u, step - 2)
-            run(minus_mean, step - 2)
-            run(spread, step - 2)
-            run(first_matmul, step - 1)
+            run(spread, step - 3)
             run(copy_x, step)
-            run(reciprocal_std, step - 2)
-            run(normalise, step - 2)
+            run(reciprocal_std, step - 3)
+            run(normalise, step - 3)
             run(quantise_x, step)
-            run(activate_hidden, step - 3)
-            run(second_matmul, step - 4)
-            run(regroup_hidden, step - 3)
-            run(add_first_bias, step - 4)
-            run(quantise_hidden, step - 3)
+            run(activate_hidden, step - 4)
+            run(minus_mean, step - 2)
+            run(first_matmul, step - 1)
+            run(second_matmul, step - 5)
+            run(regroup_hidden, step - 4)
+            run(add_first_bias, step - 5)
+            run(quantise_hidden, step - 4)
             if 1 <= step <= W2_BLOCKS:
                 n = w2_order[step - 1]
                 quantise_weight_block(w2_grouped[n], w2_codes[:, n, :], w2_scales[:, n, :])
-            run(add_other_biases, step - 4)
+            run(add_other_biases, step - 5)
             if step < W2_BLOCKS:
                 n = w2_order[step]
                 w2_grouped[n] = regroup_weight_block_on_vector(w2_raw[:, n])

@@ -138,10 +138,10 @@ def tile_hiremodule_pa_kernel(tc, x, wh1, gh, bh, wh2, bh2, out):
                 in_=grouped[:].rearrange("p c t -> p (c t)"),
             )
 
-        w1_codes = consts.tile([P, W1_PASSES, F], U32, align_bytes=64)
-        w1_scales = consts.tile([P, W1_PASSES, F], U8, align_bytes=64)
-        w2_codes = consts.tile([P, W2_BLOCKS, N_TILE], U32, align_bytes=64)
-        w2_scales = consts.tile([P, W2_BLOCKS, N_TILE], U8, align_bytes=64)
+        w1_codes = consts.tile([P, W1_PASSES, F], U32, align_bytes=256)
+        w1_scales = consts.tile([P, W1_PASSES, F], U8, align_bytes=256)
+        w2_codes = consts.tile([P, W2_BLOCKS, N_TILE], U32, align_bytes=256)
+        w2_scales = consts.tile([P, W2_BLOCKS, N_TILE], U8, align_bytes=256)
 
         x_t, x_grouped, x_codes, x_scales = {}, {}, {}, {}
         u_bank, u_rows, totals, shifts, square_sums, rstds, norms = {}, {}, {}, {}, {}, {}, {}
@@ -172,8 +172,8 @@ def tile_hiremodule_pa_kernel(tc, x, wh1, gh, bh, wh2, bh2, out):
         def quantise_x(n):
             w, j = regions[n]
             for h in new_rows(w, j):
-                codes = x_code_pool.tile([P, ROW_PASSES, P], U32, align_bytes=64, tag="x_codes")
-                scales = x_code_pool.tile([P, ROW_PASSES, P], U8, align_bytes=64, tag="x_scales")
+                codes = x_code_pool.tile([P, ROW_PASSES, P], U32, align_bytes=256, tag="x_codes")
+                scales = x_code_pool.tile([P, ROW_PASSES, P], U8, align_bytes=256, tag="x_scales")
                 nc.vector.quantize_mx(
                     out=codes[:].rearrange("p g b -> p (g b)").bitcast(FP8X4),
                     scales=scales[:].rearrange("p g b -> p (g b)"),
@@ -262,8 +262,8 @@ def tile_hiremodule_pa_kernel(tc, x, wh1, gh, bh, wh2, bh2, out):
             hid_grouped[n] = grouped
 
         def quantise_hidden(n):
-            codes = work.tile([P, P], U32, align_bytes=64, tag="hid_codes")
-            scales = work.tile([P, P], U8, align_bytes=64, tag="hid_scales")
+            codes = work.tile([P, P], U32, align_bytes=256, tag="hid_codes")
+            scales = work.tile([P, P], U8, align_bytes=256, tag="hid_scales")
             nc.vector.quantize_mx(
                 out=codes[:].bitcast(FP8X4),
                 scales=scales[:],

@@ -36,7 +36,7 @@ def image_row(j, pixel):
 
 def tile_hiremodule_pa_kernel(tc, x, wh1, gh, bh, wh2, bh2, out):
     nc = tc.nc
-    region_order = [[0, 1, 2]] * (W - 1) + [[1, 2, 0]]
+    region_order = [[0, 2, 1]] * (W - 1) + [[2, 1, 0]]
     regions = [(w, j) for w in range(W) for j in region_order[w]]
     with ExitStack() as ctx:
         ctx.enter_context(tc.manual_schedule())
@@ -45,7 +45,7 @@ def tile_hiremodule_pa_kernel(tc, x, wh1, gh, bh, wh2, bh2, out):
         stage = ctx.enter_context(tc.tile_pool(name="stage", bufs=3))
         work = ctx.enter_context(tc.tile_pool(name="work", bufs=3))
         x_code_pool = ctx.enter_context(tc.tile_pool(name="x_code_pool", bufs=2 * H))
-        out_pool = ctx.enter_context(tc.tile_pool(name="out_pool", bufs=6))
+        out_pool = ctx.enter_context(tc.tile_pool(name="out_pool", bufs=18))
         psum_x = ctx.enter_context(tc.psum_pool(name="psum_x", bufs=2))
         psum_u = ctx.enter_context(tc.psum_pool(name="psum_u", bufs=1))
         psum_h = ctx.enter_context(tc.psum_pool(name="psum_h", bufs=1))
@@ -86,11 +86,11 @@ def tile_hiremodule_pa_kernel(tc, x, wh1, gh, bh, wh2, bh2, out):
         for h in new_rows(0, 0):
             load_x(0, [h])
         load_w1(range(W1_PASSES // 2, W1_PASSES))
-        load_region(0, 1)
-        load_region(0, 2)
+        for w, j in regions[1:R]:
+            load_region(w, j)
         w2_order = [(k + W2_BLOCKS // 2) % W2_BLOCKS for k in range(W2_BLOCKS)]
         w2_raw = consts.tile([P, W2_BLOCKS, PACK, N_TILE], BF16)
-        for n, (w, j) in zip(w2_order, [(1, 0), (1, 1), (1, 2), (2, 0)]):
+        for n, (w, j) in zip(w2_order, regions[R : R + W2_BLOCKS]):
             nc.sync.dma_start(
                 out=w2_raw[:, n],
                 in_=wh2[:, n * N_TILE : (n + 1) * N_TILE].rearrange("(p t) c -> p t c", t=PACK),
@@ -98,8 +98,8 @@ def tile_hiremodule_pa_kernel(tc, x, wh1, gh, bh, wh2, bh2, out):
             load_region(w, j)
         bias2 = consts.tile([P, K1], BF16)
         nc.sync.dma_start(out=bias2[:], in_=bh2.partition_broadcast(P))
-        load_region(2, 1)
-        load_region(2, 2)
+        for w, j in regions[R + W2_BLOCKS : 3 * R]:
+            load_region(w, j)
         for w in range(3, W):
             load_x(w, list(range(H)))
 
@@ -124,7 +124,7 @@ def tile_hiremodule_pa_kernel(tc, x, wh1, gh, bh, wh2, bh2, out):
             return grouped
 
         def regroup_weight_block_on_vector(raw):
-            grouped = stage.tile([P, N_TILE, PACK], BF16, align_bytes=64, tag="w2_grouped")
+            grouped = stage.tile([P, N_TILE, PACK], BF16, align_bytes=64, tag="w_grouped")
             nc.vector.tensor_copy(
                 out=grouped[:].rearrange("p (c i) t -> p c t i", i=4),
                 in_=raw.rearrange("p t (c i) -> p c t i", i=4),
@@ -255,7 +255,8 @@ def tile_hiremodule_pa_kernel(tc, x, wh1, gh, bh, wh2, bh2, out):
 
         def regroup_hidden(n):
             grouped = work.tile([P, P, PACK], BF16, align_bytes=64, tag="hid_grouped")
-            nc.vector.tensor_copy(
+            copy = nc.scalar.copy if n % R == R - 1 else nc.vector.tensor_copy
+            copy(
                 out=grouped[:].rearrange("p (c i) t -> p c t i", i=4),
                 in_=hid_planes[n][:].rearrange("p t (c i) -> p c t i", i=4),
             )

@@ -160,14 +160,20 @@ def tile_hiremodule_pa_kernel(tc, x, wh1, gh, bh, wh2, bh2, out):
                     )
                 x_t[(w, h)] = bank
 
-        def copy_x(n):
+        def copy_x_row(n, i):
             w, j = regions[n]
-            for h in new_rows(w, j):
+            for h in new_rows(w, j)[i : i + 1]:
                 grouped = stage.tile([P, ROW_PASSES, P, 2], F32, align_bytes=64, tag="x_grouped")
                 nc.scalar.copy(
                     out=grouped[:], in_=x_t[(w, h)][:].rearrange("p (g u) b -> p g b u", u=2)
                 )
                 x_grouped[(w, h)] = grouped
+
+        def copy_first_x(n):
+            copy_x_row(n, 0)
+
+        def copy_second_x(n):
+            copy_x_row(n, 1)
 
         def quantise_x(n):
             w, j = regions[n]
@@ -335,7 +341,8 @@ def tile_hiremodule_pa_kernel(tc, x, wh1, gh, bh, wh2, bh2, out):
                 quantise_weight_block(w1_grouped[c - 1], w1_codes[:, c - 1, :], w1_scales[:, c - 1, :])
             if c == W1_PASSES // 2 - 1:
                 run(transpose_x, 0)
-                run(copy_x, 0)
+                run(copy_first_x, 0)
+                run(copy_second_x, 0)
             if c == W1_PASSES // 2:
                 run(quantise_x, 0)
         gain_cols = consts.tile([P, 2 * PACK], F32)
@@ -347,8 +354,9 @@ def tile_hiremodule_pa_kernel(tc, x, wh1, gh, bh, wh2, bh2, out):
             run(transpose_hidden, step - 4)
             run(copy_u, step - 2)
             run(spread, step - 3)
-            run(copy_x, step)
+            run(copy_first_x, step)
             run(reciprocal_std, step - 3)
+            run(copy_second_x, step)
             run(normalise, step - 3)
             run(quantise_x, step)
             run(activate_hidden, step - 4)

from contextlib import ExitStack

import concourse.mybir as mybir
from concourse.masks import make_identity

F32 = mybir.dt.float32
BF16 = mybir.dt.bfloat16
U32 = mybir.dt.uint32
U8 = mybir.dt.uint8
FP8X4 = mybir.dt.float8_e4m3fn_x4
ACT = mybir.ActivationFunctionType
ALU = mybir.AluOpType

P = 128
PACK = 4
K_PASS = P * PACK
N_TILE = 512

B, H, W, C = 128, 5, 5, 1024
PIXEL = 2
R = 3
K1 = PIXEL * C
F = C // 2
EPS = 1e-6
ROW_PASSES = C // K_PASS
W1_PASSES = K1 // K_PASS
W2_BLOCKS = K1 // N_TILE
ROW_BLOCKS = C // N_TILE

FLOPS = 2 * B * R * W * (K1 * F + F * K1)


def image_row(j, pixel):
    return (j + R * pixel + 3) % H


def tile_hiremodule_pa_kernel(tc, x, wh1, gh, bh, wh2, bh2, out):
    nc = tc.nc
    region_order = [[0, 2, 1]] * (W - 1) + [[2, 1, 0]]
    regions = [(w, j) for w in range(W) for j in region_order[w]]
    with ExitStack() as ctx:
        ctx.enter_context(tc.manual_schedule())
        consts = ctx.enter_context(tc.tile_pool(name="consts", bufs=1))
        x_pool = ctx.enter_context(tc.tile_pool(name="x_pool", bufs=1))
        stage = ctx.enter_context(tc.tile_pool(name="stage", bufs=3))
        work = ctx.enter_context(tc.tile_pool(name="work", bufs=3))
        x_code_pool = ctx.enter_context(tc.tile_pool(name="x_code_pool", bufs=2 * H))
        out_pool = ctx.enter_context(tc.tile_pool(name="out_pool", bufs=18))
        psum_x = ctx.enter_context(tc.psum_pool(name="psum_x", bufs=2))
        psum_u = ctx.enter_context(tc.psum_pool(name="psum_u", bufs=1))
        psum_h = ctx.enter_context(tc.psum_pool(name="psum_h", bufs=1))
        psum_y = ctx.enter_context(tc.psum_pool(name="psum_y", bufs=4))

        def new_rows(w, j):
            earlier = region_order[w][: region_order[w].index(j)]
            read = [image_row(i, pixel) for i in earlier for pixel in range(PIXEL)]
            rows = [image_row(j, pixel) for pixel in range(PIXEL)]
            return [h for h in rows if h not in read]

        x_rows = {}

        def load_x(w, rows):
            step = rows[1] - rows[0] if len(rows) > 1 else 1
            x_part = x_pool.tile([P, len(rows), C], BF16, tag="x_%d_%d" % (w, rows[0]))
            nc.sync.dma_start(out=x_part[:], in_=x[:, rows[0] : rows[-1] + 1 : step, w, :])
            for i, h in enumerate(rows):
                x_rows[(w, h)] = x_part[:, i, :]

        def load_region(w, j):
            load_x(w, sorted(new_rows(w, j)))

        gain_raw = consts.tile([P, PACK], BF16)
        nc.scalar.dma_start(out=gain_raw[:], in_=gh.rearrange("(p t) -> p t", t=PACK))
        shift_raw = consts.tile([P, PACK], BF16)
        nc.scalar.dma_start(out=shift_raw[:], in_=bh.rearrange("(p t) -> p t", t=PACK))
        w1_raw = consts.tile([P, W1_PASSES, PACK, F], BF16)

        def load_w1(passes):
            for c in passes:
                nc.sync.dma_start(
                    out=w1_raw[:, c],
                    in_=wh1[c * K_PASS : (c + 1) * K_PASS, :].rearrange("(p t) f -> p t f", t=PACK),
                )

        load_w1(range(W1_PASSES // 2))
        for h in new_rows(0, 0):
            load_x(0, [h])
        load_w1(range(W1_PASSES // 2, W1_PASSES))
        for w, j in regions[1:R]:
            load_region(w, j)
        w2_order = [(k + W2_BLOCKS // 2) % W2_BLOCKS for k in range(W2_BLOCKS)]
        w2_raw = consts.tile([P, W2_BLOCKS, PACK, N_TILE], BF16)
        for n, (w, j) in zip(w2_order, regions[R : R + W2_BLOCKS]):
            nc.sync.dma_start(
                out=w2_raw[:, n],
                in_=wh2[:, n * N_TILE : (n + 1) * N_TILE].rearrange("(p t) c -> p t c", t=PACK),
            )
            load_region(w, j)
        bias2 = consts.tile([P, K1], BF16)
        nc.sync.dma_start(out=bias2[:], in_=bh2.partition_broadcast(P))
        for w, j in regions[R + W2_BLOCKS : 3 * R]:
            load_region(w, j)
        for w in range(3, W):
            load_x(w, list(range(H)))

        ident = consts.tile([P, P], F32)
        make_identity(nc, ident[:])
        eps = consts.tile([P, 1], F32)
        nc.vector.memset(eps[:], EPS)
        warm = consts.tile([P, 1], F32)
        nc.scalar.activation(out=warm[:], in_=eps[:], func=ACT.Abs_reciprocal_sqrt, bias=eps[:])

        def regroup_weight_block(raw):
            grouped = stage.tile([P, N_TILE, PACK], BF16, align_bytes=64, tag="w_grouped")
            half = N_TILE // 2
            nc.vector.tensor_copy(
                out=grouped[:, :half, :].rearrange("p (c i) t -> p c t i", i=4),
                in_=raw[:, :, :half].rearrange("p t (c i) -> p c t i", i=4),
            )
            nc.scalar.copy(
                out=grouped[:, half:, :].rearrange("p (c i) t -> p c t i", i=4),
                in_=raw[:, :, half:].rearrange("p t (c i) -> p c t i", i=4),
            )
            return grouped

        def regroup_weight_block_on_vector(raw):
            grouped = stage.tile([P, N_TILE, PACK], BF16, align_bytes=64, tag="w_grouped")
            nc.vector.tensor_copy(
                out=grouped[:].rearrange("p (c i) t -> p c t i", i=4),
                in_=raw.rearrange("p t (c i) -> p c t i", i=4),
            )
            return grouped

        def quantise_weight_block(grouped, codes, scales):
            nc.vector.quantize_mx(
                out=codes.bitcast(FP8X4),
                scales=scales,
                in_=grouped[:].rearrange("p c t -> p (c t)"),
            )

        w1_codes = consts.tile([P, W1_PASSES, F], U32, align_bytes=256)
        w1_scales = consts.tile([P, W1_PASSES, F], U8, align_bytes=256)
        w2_codes = consts.tile([P, W2_BLOCKS, N_TILE], U32, align_bytes=256)
        w2_scales = consts.tile([P, W2_BLOCKS, N_TILE], U8, align_bytes=256)

        x_t, x_grouped, x_codes, x_scales = {}, {}, {}, {}
        u_bank, u_rows, totals, shifts, square_sums, rstds, norms = {}, {}, {}, {}, {}, {}, {}
        hid_ts, hid_planes, hid_grouped, hid_codes, hid_scales = {}, {}, {}, {}, {}
        y_bank, results = {}, {}

        def transpose_x(n):
            w, j = regions[n]
            for h in new_rows(w, j):
                x_words = x_rows[(w, h)].bitcast(F32)
                bank = psum_x.tile([P, 2 * ROW_PASSES, P], F32)
                for q in range(2 * ROW_PASSES):
                    first = (q // 2) * 2 * P + q % 2
                    nc.tensor.transpose(
                        bank[:, q, :], x_words[:, first : first + 2 * P - 1 : 2], ident[:]
                    )
                x_t[(w, h)] = bank

        def copy_x_row(n, i):
            w, j = regions[n]
            for h in new_rows(w, j)[i : i + 1]:
                grouped = stage.tile([P, ROW_PASSES, P, 2], F32, align_bytes=64, tag="x_grouped")
                nc.scalar.copy(
                    out=grouped[:], in_=x_t[(w, h)][:].rearrange("p (g u) b -> p g b u", u=2)
                )
                x_grouped[(w, h)] = grouped

        def copy_first_x(n):
            copy_x_row(n, 0)

        def copy_second_x(n):
            copy_x_row(n, 1)

        def quantise_x(n):
            w, j = regions[n]
            for h in new_rows(w, j):
                codes = x_code_pool.tile([P, ROW_PASSES, P], U32, align_bytes=256, tag="x_codes")
                scales = x_code_pool.tile([P, ROW_PASSES, P], U8, align_bytes=256, tag="x_scales")
                nc.vector.quantize_mx(
                    out=codes[:].rearrange("p g b -> p (g b)").bitcast(FP8X4),
                    scales=scales[:].rearrange("p g b -> p (g b)"),
                    in_=x_grouped[(w, h)][:].rearrange("p g b u -> p (g b u)").bitcast(BF16),
                )
                x_codes[(w, h)], x_scales[(w, h)] = codes, scales

        def first_matmul(n):
            w, j = regions[n]
            u = psum_u.tile([P, F], F32)
            for c in range(W1_PASSES):
                h = image_row(j, c // ROW_PASSES)
                g = c % ROW_PASSES
                nc.tensor.matmul_mx(
                    out=u[:],
                    lhsT=x_codes[(w, h)][:, g, :].bitcast(FP8X4),
                    lhsT_scale=x_scales[(w, h)][:, g, :],
                    rhs=w1_codes[:, c, :].bitcast(FP8X4),
                    rhs_scale=w1_scales[:, c, :],
                    start=(c == 0),
                    stop=(c == W1_PASSES - 1),
                )
            u_bank[n] = u

        def copy_u(n):
            u_row = work.tile([P, F], F32)
            total = work.tile([P, 1], F32)
            nc.scalar.activation(
                out=u_row[:].rearrange("p (t m) -> p t m", t=PACK),
                in_=u_bank[n][:].rearrange("p (m t) -> p t m", t=PACK),
                func=ACT.Identity, accum_out=total[:],
            )
            u_rows[n], totals[n] = u_row, total

        def minus_mean(n):
            shift = work.tile([P, 1], F32)
            nc.scalar.mul(out=shift[:], in_=totals[n][:], mul=-1.0 / F)
            shifts[n] = shift

        def spread(n):
            squares = work.tile([P, F], BF16)
            square_sum = work.tile([P, 1], F32)
            nc.scalar.activation(
                out=squares[:], in_=u_rows[n][:], func=ACT.Square, bias=shifts[n][:],
                accum_out=square_sum[:],
            )
            square_sums[n] = square_sum

        def reciprocal_std(n):
            rstd = work.tile([P, 1], F32)
            nc.scalar.activation(
                out=rstd[:], in_=square_sums[n][:], func=ACT.Abs_reciprocal_sqrt,
                scale=1.0 / F, bias=eps[:],
            )
            rstds[n] = rstd

        def normalise(n):
            norm = work.tile([P, F], F32)
            nc.vector.tensor_scalar(
                out=norm[:], in0=u_rows[n][:], scalar1=shifts[n][:], scalar2=rstds[n][:],
                op0=ALU.add, op1=ALU.mult,
            )
            norms[n] = norm

        def transpose_hidden(n):
            hid_t = psum_h.tile([P, PACK, P], F32, tag="hid_t")
            for t in range(PACK):
                nc.tensor.transpose(hid_t[:, t, :], norms[n][:, t * P : (t + 1) * P], ident[:])
            hid_ts[n] = hid_t

        def activate_hidden(n):
            planes = work.tile([P, PACK, P], BF16)
            for t in range(PACK):
                nc.scalar.activation(
                    out=planes[:, t, :], in_=hid_ts[n][:, t, :], func=ACT.Relu,
                    scale=gain_cols[:, t : t + 1], bias=gain_cols[:, PACK + t : PACK + t + 1],
                )
            hid_planes[n] = planes

        def regroup_hidden(n):
            grouped = work.tile([P, P, PACK], BF16, align_bytes=64, tag="hid_grouped")
            copy = nc.scalar.copy if n % R == R - 1 else nc.vector.tensor_copy
            copy(
                out=grouped[:].rearrange("p (c i) t -> p c t i", i=4),
                in_=hid_planes[n][:].rearrange("p t (c i) -> p c t i", i=4),
            )
            hid_grouped[n] = grouped

        def quantise_hidden(n):
            codes = work.tile([P, P], U32, align_bytes=256, tag="hid_codes")
            scales = work.tile([P, P], U8, align_bytes=256, tag="hid_scales")
            nc.vector.quantize_mx(
                out=codes[:].bitcast(FP8X4),
                scales=scales[:],
                in_=hid_grouped[n][:].rearrange("p b t -> p (b t)"),
            )
            hid_codes[n], hid_scales[n] = codes, scales

        def banks(n):
            first_pixel = 1 if regions[n][1] == 0 else 0
            return [(pixel, half) for pixel in range(first_pixel, PIXEL) for half in range(ROW_BLOCKS)]

        def second_matmul(n):
            for pixel, half in banks(n):
                block = pixel * ROW_BLOCKS + half
                y = psum_y.tile([P, N_TILE], F32)
                nc.tensor.matmul_mx(
                    out=y[:],
                    lhsT=hid_codes[n][:].bitcast(FP8X4),
                    lhsT_scale=hid_scales[n][:],
                    rhs=w2_codes[:, block, :].bitcast(FP8X4),
                    rhs_scale=w2_scales[:, block, :],
                    start=True,
                    stop=True,
                )
                y_bank[(n, pixel, half)] = y

        def add_bias(n, some_banks):
            w, j = regions[n]
            for pixel, half in some_banks:
                block = pixel * ROW_BLOCKS + half
                if half == 0:
                    result = out_pool.tile([P, C], F32)
                    results[(n, pixel)] = result
                columns = results[(n, pixel)][:, half * N_TILE : (half + 1) * N_TILE]
                nc.vector.tensor_tensor(
                    out=columns,
                    in0=y_bank[(n, pixel, half)][:],
                    in1=bias2[:, block * N_TILE : (block + 1) * N_TILE],
                    op=ALU.add,
                )
                row = out[:, image_row(j, pixel), w, :]
                if n == len(regions) - 1:
                    nc.sync.dma_start(out=row[:, half * N_TILE : (half + 1) * N_TILE], in_=columns)
                elif half == ROW_BLOCKS - 1:
                    nc.sync.dma_start(out=row, in_=results[(n, pixel)][:])

        def add_first_bias(n):
            add_bias(n, banks(n)[:1])

        def add_other_biases(n):
            add_bias(n, banks(n)[1:])

        def run(stage_of_region, n):
            if 0 <= n < len(regions):
                stage_of_region(n)

        def keep_tensor_busy(rows):
            y = psum_y.tile([P, N_TILE], F32)
            for repeat in range(2):
                nc.tensor.matmul(y[:], lhsT=rows[:, :P], rhs=rows, start=True, stop=True)

        w1_grouped = {}
        for c in range(W1_PASSES + 1):
            if c < W1_PASSES:
                w1_grouped[c] = regroup_weight_block(w1_raw[:, c])
                keep_tensor_busy(w1_raw[:, c, 0, :])
            if c > 0:
                quantise_weight_block(w1_grouped[c - 1], w1_codes[:, c - 1, :], w1_scales[:, c - 1, :])
            if c == W1_PASSES // 2 - 1:
                run(transpose_x, 0)
                run(copy_first_x, 0)
                run(copy_second_x, 0)
            if c == W1_PASSES // 2:
                run(quantise_x, 0)
        gain_cols = consts.tile([P, 2 * PACK], F32)
        nc.vector.tensor_copy(out=gain_cols[:, 0:PACK], in_=gain_raw[:])
        nc.vector.tensor_copy(out=gain_cols[:, PACK : 2 * PACK], in_=shift_raw[:])
        w2_grouped = {w2_order[0]: regroup_weight_block_on_vector(w2_raw[:, w2_order[0]])}
        for step in range(1, len(regions) + 5):
            run(transpose_x, step)
            run(transpose_hidden, step - 4)
            run(copy_u, step - 2)
            run(spread, step - 3)
            run(copy_first_x, step)
            run(reciprocal_std, step - 3)
            run(copy_second_x, step)
            run(normalise, step - 3)
            run(quantise_x, step)
            run(activate_hidden, step - 4)
            run(minus_mean, step - 2)
            run(first_matmul, step - 1)
            run(second_matmul, step - 5)
            run(regroup_hidden, step - 4)
            run(add_first_bias, step - 5)
            run(quantise_hidden, step - 4)
            if 1 <= step <= W2_BLOCKS:
                n = w2_order[step - 1]
                quantise_weight_block(w2_grouped[n], w2_codes[:, n, :], w2_scales[:, n, :])
            run(add_other_biases, step - 5)
            if step < W2_BLOCKS:
                n = w2_order[step]
                w2_grouped[n] = regroup_weight_block_on_vector(w2_raw[:, n])
